import numpy as np
import ml_dtypes


def mxq(x, axis, fmt="e4m3"):
    dtype, down = {"e4m3": (ml_dtypes.float8_e4m3fn, 7), "e5m2": (ml_dtypes.float8_e5m2, 14)}[fmt]
    v = np.moveaxis(np.asarray(x, np.float32).astype(ml_dtypes.bfloat16).astype(np.float64), axis, -1)
    blocks = v.reshape(v.shape[:-1] + (-1, 32))
    amax = np.abs(blocks).max(-1, keepdims=True)
    byte = np.maximum(np.where(amax > 0, np.frexp(amax)[1] - 1 + 127, 0) - down, 1)
    scale = np.exp2(byte - 127.0)
    codes = (blocks / scale).astype(np.float32).astype(dtype).astype(np.float64)
    return np.moveaxis((codes * scale).reshape(v.shape), -1, axis)


WIDE = False


def mx_kscale(k):
    if not WIDE:
        return np.ones(k)
    levels = np.array([10, -10, 5, -5, 0])
    a = np.random.permutation(np.resize(levels, k // 512 * 4)).reshape(k // 512, 4)
    idx = np.arange(k)
    return np.exp2(a[idx // 512, idx % 128 // 32])


BF16 = ml_dtypes.bfloat16


def bf(x):
    return np.asarray(x, np.float32).astype(BF16)


def f64(x):
    return np.asarray(x).astype(np.float64)


E2M1 = np.array([0.0, 0.5, 1.0, 1.5, 2.0, 3.0, 4.0, 6.0, -0.0, -0.5, -1.0, -1.5, -2.0, -3.0, -4.0, -6.0])


def pack_weight(w, fmt):
    k, n = w.shape
    w = f64(bf(w)).reshape(k // 32, 32, n)
    amax = np.abs(w).max(1)
    if fmt == "e4m3":
        byte = np.frexp(amax)[1] - 1 + 127 - 7
    else:
        mant, ex = np.frexp(amax / 6.0)
        byte = np.where(mant > 0.5, ex, ex - 1) + 127
    byte = np.clip(np.where(amax > 0, byte, 1), 1, 254)
    scaled = (w * np.exp2(127.0 - byte)[:, None, :]).reshape(k, n).astype(np.float32)
    by_word = np.ascontiguousarray(scaled.reshape(k // 512, 128, 4, n).transpose(0, 1, 3, 2))
    if fmt == "e4m3":
        words = by_word.astype(ml_dtypes.float8_e4m3fn).view(np.uint8)
    else:
        c = by_word.astype(ml_dtypes.float4_e2m1fn).view(np.uint8) & 0xF
        words = c[..., 0::2] | (c[..., 1::2] << 4)
    return np.ascontiguousarray(words), np.ascontiguousarray(byte.astype(np.uint8).reshape(k // 512, 16, n))


def unpack_weight(words, scales, fmt):
    g, p, n, _ = words.shape
    if fmt == "e4m3":
        vals = np.ascontiguousarray(words).view(ml_dtypes.float8_e4m3fn).astype(np.float64)
    else:
        nib = np.empty((g, p, n, 4), np.uint8)
        nib[..., 0::2] = words & 0xF
        nib[..., 1::2] = words >> 4
        vals = E2M1[nib]
    vals = vals * np.repeat(np.exp2(scales.astype(np.float64) - 127.0), 8, axis=1)[..., None]
    return vals.transpose(0, 1, 3, 2).reshape(g * 512, n)

def pack4(w):
    words, scales = pack_weight(w, "e2m1")
    return words.reshape(words.shape[0], 128, -1), scales


def unpack4(words, scales):
    return unpack_weight(words.reshape(words.shape[0], 128, -1, 2), scales, "e2m1")


B, S, E, H, KD, HD, C = 1, 128, 16384, 8, 128, 256, 512
W = H * KD


def angles():
    lin = np.linspace(0.0, 1.0, KD // 2)
    angle = np.repeat(1.0 / (10000.0 ** lin), 2)
    idx = np.arange(S, dtype=np.float64)
    return np.sin(idx[:, None] * angle[None, :]), np.cos(idx[:, None] * angle[None, :])


def rotate_every_two(t):
    t1 = t[..., ::2]
    t2 = t[..., 1::2]
    return np.stack((-t2, t1), axis=-1).reshape(t.shape)


def setup_inputs():
    s = mx_kscale(E)
    x = bf(np.random.standard_normal((B, S, E)) * s)
    wq_words, wq_scales = pack4(np.random.standard_normal((E, W)) * 1.4 / np.sqrt(E) / s[:, None])
    wk_words, wk_scales = pack4(np.random.standard_normal((E, W)) * 1.4 / np.sqrt(E) / s[:, None])
    return {"x": x,
            "wq_words": wq_words, "wq_scales": wq_scales,
            "wk_words": wk_words, "wk_scales": wk_scales}


def reference(x, wq_words, wq_scales, wk_words, wk_scales):
    sin, cos = angles()
    xq = mxq(f64(x), 2, "e4m3")
    q = xq @ unpack4(wq_words, wq_scales)
    k = (xq @ unpack4(wk_words, wk_scales)) * KD ** -0.5
    q = q.reshape(B, S, H, KD).transpose(0, 2, 1, 3)
    k = k.reshape(B, S, H, KD).transpose(0, 2, 1, 3)
    q_rot = q * cos + rotate_every_two(q) * sin
    k_rot = k * cos + rotate_every_two(k) * sin
    return q_rot, k_rot

@@ -1,0 +1,230 @@
+import math
+from contextlib import ExitStack
+
+import concourse.mybir as mybir
+from concourse.masks import make_identity
+
+F32 = mybir.dt.float32
+BF16 = mybir.dt.bfloat16
+I32 = mybir.dt.int32
+U32 = mybir.dt.uint32
+U8 = mybir.dt.uint8
+FP8X4 = mybir.dt.float8_e4m3fn_x4
+FP4X4 = mybir.dt.float4_e2m1fn_x4
+ALU = mybir.AluOpType
+ACT = mybir.ActivationFunctionType
+
+P = 128
+E = 16384
+K_PASS = 512
+GROUPS = E // K_PASS
+WIDTH = 1024
+N_PASS = 512
+BANKS = WIDTH // N_PASS
+HEAD = 128
+HEADS_PER_BANK = N_PASS // HEAD
+PAIRS = HEAD // 2
+
+X_LOADS = 8
+UNIT = 2
+UNITS = GROUPS // UNIT
+CHUNK = 2
+CHUNKS = GROUPS // CHUNK
+RING = 18
+SCALE_ROWS = 4
+
+FLOPS = 2 * P * E * 2 * WIDTH
+
+ROUND_MAGIC = 12582912.0
+TURN_HI = 6.28125
+TURN_LO = 2.0 * math.pi - TURN_HI
+
+
+def tile_retnet_pa_k_kernel(
+    tc, x, wq_words, wq_scales, wk_words, wk_scales, out_0, out_1
+):
+    nc = tc.nc
+    words_in = (wq_words, wk_words)
+    scales_in = (wq_scales, wk_scales)
+    outs = (out_0, out_1)
+    factors = (1.0, HEAD**-0.5)
+
+    with ExitStack() as stack:
+        keep = stack.enter_context(tc.tile_pool(name="keep", bufs=1))
+        stage = stack.enter_context(tc.tile_pool(name="stage", bufs=4))
+        ring = stack.enter_context(tc.tile_pool(name="ring", bufs=RING))
+        work = stack.enter_context(tc.tile_pool(name="work", bufs=2))
+        psum_t = stack.enter_context(tc.psum_pool(name="psum_t", bufs=4))
+        psum_acc = stack.enter_context(tc.psum_pool(name="psum_acc", bufs=1))
+        stack.enter_context(tc.manual_schedule())
+
+        ident = keep.tile([P, P], F32)
+        make_identity(nc, ident[:])
+        pos_int = keep.tile([P, 1], I32)
+        nc.gpsimd.iota(pos_int[:], pattern=[[0, 1]], base=0, channel_multiplier=1)
+
+        planes = []
+        for w in range(2):
+            plane = keep.tile([P, GROUPS, WIDTH], U8, align_bytes=64, name="plane%d" % w)
+            nc.vector.memset(plane[:].bitcast(I32), 0)
+            planes.append(plane)
+
+        def load_scale_rows(w, r):
+            rows = scales_in[w].bitcast(I32).rearrange("g (a r) n -> r a g n", r=SCALE_ROWS)
+            nc.sync.dma_start(out=planes[w][r:P:32, :, :].bitcast(I32), in_=rows[r])
+
+        x_raw = keep.tile([P, E], BF16)
+        x_block = E // X_LOADS
+        for j in range(X_LOADS):
+            cols = slice(j * x_block, (j + 1) * x_block)
+            nc.sync.dma_start(out=x_raw[:, cols], in_=x[0, :, cols])
+        x_pairs = x_raw[:].bitcast(F32)
+
+        x_codes = keep.tile([P, GROUPS * P], U32, align_bytes=64)
+        x_scales = keep.tile([P, GROUPS * P], U8, align_bytes=64)
+
+        def transpose_and_quantise(unit):
+            turned = psum_t.tile([P, UNIT * 2 * P], F32)
+            for i in range(UNIT):
+                g = unit * UNIT + i
+                for u in range(2):
+                    at = (i * 2 + u) * P
+                    nc.tensor.transpose(
+                        out=turned[:, at : at + P],
+                        in_=x_pairs[:, 256 * g + u : 256 * (g + 1) : 2],
+                        identity=ident[:],
+                    )
+            grouped = stage.tile([P, UNIT * P * 4], BF16, align_bytes=64)
+            nc.scalar.copy(
+                out=grouped[:].bitcast(F32).rearrange("p (i r u) -> p i r u", i=UNIT, u=2),
+                in_=turned[:].rearrange("p (i u r) -> p i r u", i=UNIT, u=2),
+            )
+            cols = slice(unit * UNIT * P, (unit + 1) * UNIT * P)
+            nc.vector.quantize_mx(
+                out=x_codes[:, cols].bitcast(FP8X4), scales=x_scales[:, cols], in_=grouped[:]
+            )
+
+        for unit in range(UNITS):
+            transpose_and_quantise(unit)
+
+        freq = keep.tile([P, PAIRS], F32)
+        nc.vector.memset(freq[:], 1.0)
+        for bit in range(6):
+            step = 1 << bit
+            odd = freq[:].rearrange("p (a two s) -> p a two s", two=2, s=step)[:, :, 1, :]
+            nc.vector.tensor_scalar_mul(out=odd, in0=odd, scalar1=10000.0 ** (-step / 63.0))
+        pos = keep.tile([P, 1], F32)
+        nc.vector.tensor_copy(out=pos[:], in_=pos_int[:])
+        angle = keep.tile([P, 2, PAIRS], F32)
+        nc.vector.tensor_scalar_mul(out=angle[:, 0, :], in0=freq[:], scalar1=pos[:, 0:1])
+        nc.vector.tensor_scalar(
+            out=angle[:, 1, :], in0=freq[:], scalar1=pos[:, 0:1], scalar2=math.pi / 2,
+            op0=ALU.mult, op1=ALU.add,
+        )
+        flat_angle = angle[:].rearrange("p a c -> p (a c)")
+        turns = keep.tile([P, 2 * PAIRS], F32)
+        nc.vector.tensor_scalar(
+            out=turns[:], in0=flat_angle, scalar1=1.0 / (2.0 * math.pi), scalar2=ROUND_MAGIC,
+            op0=ALU.mult, op1=ALU.add,
+        )
+        nc.vector.tensor_scalar_sub(out=turns[:], in0=turns[:], scalar1=ROUND_MAGIC)
+        nc.vector.scalar_tensor_tensor(
+            out=flat_angle, in0=turns[:], scalar=-TURN_HI, in1=flat_angle,
+            op0=ALU.mult, op1=ALU.add,
+        )
+        nc.vector.scalar_tensor_tensor(
+            out=flat_angle, in0=turns[:], scalar=-TURN_LO, in1=flat_angle,
+            op0=ALU.mult, op1=ALU.add,
+        )
+        trig = keep.tile([P, 2, PAIRS], F32)
+        nc.scalar.activation(
+            out=trig[:].rearrange("p a c -> p (a c)"), in_=flat_angle, func=ACT.Sin
+        )
+        cos_tab, sin_tab, neg_sin_tab = [], [], []
+        for w in range(2):
+            cos_w = keep.tile([P, HEAD], F32, name="cos%d" % w)
+            sin_w = keep.tile([P, PAIRS], F32, name="sin%d" % w)
+            neg_w = keep.tile([P, PAIRS], F32, name="neg%d" % w)
+            nc.vector.tensor_scalar_mul(
+                out=cos_w[:].rearrange("p (c e) -> p c e", e=2),
+                in0=trig[:, 1, :].unsqueeze(2).to_broadcast([P, PAIRS, 2]),
+                scalar1=factors[w],
+            )
+            nc.vector.tensor_scalar_mul(out=sin_w[:], in0=trig[:, 0, :], scalar1=factors[w])
+            nc.vector.tensor_scalar_mul(out=neg_w[:], in0=trig[:, 0, :], scalar1=-factors[w])
+            cos_tab.append(cos_w)
+            sin_tab.append(sin_w)
+            neg_sin_tab.append(neg_w)
+
+        acc = [
+            [psum_acc.tile([P, N_PASS], F32, name="acc%d%d" % (w, b)) for b in range(BANKS)]
+            for w in range(2)
+        ]
+        loaded = {}
+
+        def load_words(step):
+            w, chunk = divmod(step, CHUNKS)
+            words = ring.tile([P, CHUNK, 2 * WIDTH], U8, align_bytes=64)
+            src = words_in[w][chunk * CHUNK : (chunk + 1) * CHUNK].bitcast(I32)
+            nc.sync.dma_start(out=words[:].bitcast(I32), in_=src.rearrange("g p n -> p g n"))
+            loaded[step] = words
+
+        def multiply(step):
+            w, chunk = divmod(step, CHUNKS)
+            words = loaded[step]
+            for b in range(BANKS):
+                for i in range(CHUNK):
+                    g = chunk * CHUNK + i
+                    nc.tensor.matmul_mx(
+                        out=acc[w][b][:],
+                        lhsT=x_codes[:, g * P : (g + 1) * P].bitcast(FP8X4),
+                        lhsT_scale=x_scales[:, g * P : (g + 1) * P],
+                        rhs=words[:, i, b * 2 * N_PASS : (b + 1) * 2 * N_PASS].bitcast(FP4X4),
+                        rhs_scale=planes[w][:, g, b * N_PASS : (b + 1) * N_PASS],
+                        start=(g == 0),
+                        stop=(g == GROUPS - 1),
+                    )
+
+        def rotate_and_store(w, b):
+            t = acc[w][b][:]
+            by_pair = t.rearrange("p (h c e) -> p h c e", h=HEADS_PER_BANK, e=2)
+            direct = work.tile([P, N_PASS], F32)
+            nc.vector.tensor_tensor(
+                out=direct[:].rearrange("p (h f) -> p h f", h=HEADS_PER_BANK),
+                in0=t.rearrange("p (h f) -> p h f", h=HEADS_PER_BANK),
+                in1=cos_tab[w][:].unsqueeze(1).to_broadcast([P, HEADS_PER_BANK, HEAD]),
+                op=ALU.mult,
+            )
+            crossed = work.tile([P, 2, N_PASS // 2], F32)
+            for e, table in ((0, neg_sin_tab[w]), (1, sin_tab[w])):
+                nc.vector.tensor_tensor(
+                    out=crossed[:, e, :].rearrange("p (h c) -> p h c", h=HEADS_PER_BANK),
+                    in0=by_pair[:, :, :, 1 - e],
+                    in1=table[:].unsqueeze(1).to_broadcast([P, HEADS_PER_BANK, PAIRS]),
+                    op=ALU.mult,
+                )
+            rotated = work.tile([P, N_PASS], F32)
+            nc.vector.tensor_tensor(
+                out=rotated[:].rearrange("p (m e) -> p m e", e=2),
+                in0=direct[:].rearrange("p (m e) -> p m e", e=2),
+                in1=crossed[:].rearrange("p e m -> p m e"),
+                op=ALU.add,
+            )
+            heads = slice(b * HEADS_PER_BANK, (b + 1) * HEADS_PER_BANK)
+            nc.scalar.dma_start(
+                out=outs[w][0, heads].rearrange("h i f -> i h f"),
+                in_=rotated[:].rearrange("p (h f) -> p h f", h=HEADS_PER_BANK),
+            )
+
+        ahead = RING - 1
+        for step in range(2 * CHUNKS + ahead):
+            if step < 2 * SCALE_ROWS:
+                load_scale_rows(step // SCALE_ROWS, step % SCALE_ROWS)
+            if step < 2 * CHUNKS:
+                load_words(step)
+            done = step - ahead
+            if done >= 0:
+                multiply(done)
+                if done % CHUNKS == CHUNKS - 1:
+                    for b in range(BANKS):
+                        rotate_and_store(done // CHUNKS, b)

@@ -31,7 +31,7 @@ UNITS = GROUPS // UNIT
 CHUNK = 2
 CHUNKS = GROUPS // CHUNK
 RING = 18
-SCALE_ROWS = 4
+SCALE_LOADS = 8
 
 FLOPS = 2 * P * E * 2 * WIDTH
 
@@ -69,9 +69,10 @@ def tile_retnet_pa_k_kernel(
             nc.vector.memset(plane[:].bitcast(I32), 0)
             planes.append(plane)
 
-        def load_scale_rows(w, r):
-            rows = scales_in[w].bitcast(I32).rearrange("g (a r) n -> r a g n", r=SCALE_ROWS)
-            nc.sync.dma_start(out=planes[w][r:P:32, :, :].bitcast(I32), in_=rows[r])
+        def load_scale_rows(w, q):
+            rows = scales_in[w].bitcast(I32).rearrange("g (h q) n -> q h g n", h=2)
+            first = 32 * (q // 4) + q % 4
+            nc.sync.dma_start(out=planes[w][first:P:64, :, :].bitcast(I32), in_=rows[q])
 
         x_raw = keep.tile([P, E], BF16)
         x_block = E // X_LOADS
@@ -218,8 +219,8 @@ def tile_retnet_pa_k_kernel(
 
         ahead = RING - 1
         for step in range(2 * CHUNKS + ahead):
-            if step < 2 * SCALE_ROWS:
-                load_scale_rows(step // SCALE_ROWS, step % SCALE_ROWS)
+            if step < 2 * SCALE_LOADS:
+                load_scale_rows(step // SCALE_LOADS, step % SCALE_LOADS)
             if step < 2 * CHUNKS:
                 load_words(step)
             done = step - ahead

@@ -31,7 +31,7 @@ UNITS = GROUPS // UNIT
 CHUNK = 2
 CHUNKS = GROUPS // CHUNK
 RING = 18
-SCALE_LOADS = 8
+BLOCKS = K_PASS // 32
 
 FLOPS = 2 * P * E * 2 * WIDTH
 
@@ -69,10 +69,14 @@ def tile_retnet_pa_k_kernel(
             nc.vector.memset(plane[:].bitcast(I32), 0)
             planes.append(plane)
 
-        def load_scale_rows(w, q):
-            rows = scales_in[w].bitcast(I32).rearrange("g (h q) n -> q h g n", h=2)
-            first = 32 * (q // 4) + q % 4
-            nc.sync.dma_start(out=planes[w][first:P:64, :, :].bitcast(I32), in_=rows[q])
+        def load_scales(w):
+            rows = scales_in[w].bitcast(I32).rearrange("g q n -> q g n")
+            for i in range(BLOCKS):
+                q = (i % 2) * (BLOCKS // 2) + i // 2
+                at = 32 * (q // 4) + q % 4
+                nc.sync.dma_start(
+                    out=planes[w][at : at + 1, :, :].bitcast(I32), in_=rows[q : q + 1]
+                )
 
         x_raw = keep.tile([P, E], BF16)
         x_block = E // X_LOADS
@@ -218,9 +222,10 @@ def tile_retnet_pa_k_kernel(
             )
 
         ahead = RING - 1
+        load_scales(0)
         for step in range(2 * CHUNKS + ahead):
-            if step < 2 * SCALE_LOADS:
-                load_scale_rows(step // SCALE_LOADS, step % SCALE_LOADS)
+            if step == CHUNKS // 2:
+                load_scales(1)
             if step < 2 * CHUNKS:
                 load_words(step)
             done = step - ahead

@@ -16,8 +16,10 @@ ACT = mybir.ActivationFunctionType
 
 P = 128
 E = 16384
+BLOCK = 32
 K_PASS = 512
-GROUPS = E // K_PASS
+PASSES = E // K_PASS
+STRETCHES = K_PASS // BLOCK
 WIDTH = 1024
 N_PASS = 512
 BANKS = WIDTH // N_PASS
@@ -27,11 +29,8 @@ PAIRS = HEAD // 2
 
 X_LOADS = 8
 UNIT = 2
-UNITS = GROUPS // UNIT
-CHUNK = 2
-CHUNKS = GROUPS // CHUNK
-RING = 18
-BLOCKS = K_PASS // 32
+UNITS = PASSES // UNIT
+RING = 24
 
 FLOPS = 2 * P * E * 2 * WIDTH
 
@@ -65,38 +64,45 @@ def tile_retnet_pa_k_kernel(
 
         planes = []
         for w in range(2):
-            plane = keep.tile([P, GROUPS, WIDTH], U8, align_bytes=64, name="plane%d" % w)
+            plane = keep.tile([P, PASSES * WIDTH], U8, align_bytes=64, name="plane%d" % w)
             nc.vector.memset(plane[:].bitcast(I32), 0)
             planes.append(plane)
 
         def load_scales(w):
-            rows = scales_in[w].bitcast(I32).rearrange("g q n -> q g n")
-            for i in range(BLOCKS):
-                q = (i % 2) * (BLOCKS // 2) + i // 2
-                at = 32 * (q // 4) + q % 4
-                nc.sync.dma_start(
-                    out=planes[w][at : at + 1, :, :].bitcast(I32), in_=rows[q : q + 1]
-                )
+            rows = scales_in[w].bitcast(I32).rearrange("g q n -> (g q) n")
+            rows = rows.rearrange("(h a j) n -> a h (j n)", h=2, j=PASSES)
+            for a in range(STRETCHES // 2):
+                first = 32 * (a // 4) + a % 4
+                nc.sync.dma_start(out=planes[w][first:P:64, :].bitcast(I32), in_=rows[a])
 
         x_raw = keep.tile([P, E], BF16)
-        x_block = E // X_LOADS
-        for j in range(X_LOADS):
-            cols = slice(j * x_block, (j + 1) * x_block)
+        x_sorted = keep.tile([P, E], BF16)
+        by_pass = x_sorted[:].rearrange("p (j a e) -> p j a e", j=PASSES, e=BLOCK)
+        x_cols = E // X_LOADS
+        per_load = STRETCHES // X_LOADS
+        for c in range(X_LOADS):
+            cols = slice(c * x_cols, (c + 1) * x_cols)
             nc.sync.dma_start(out=x_raw[:, cols], in_=x[0, :, cols])
-        x_pairs = x_raw[:].bitcast(F32)
+        for c in range(X_LOADS):
+            cols = slice(c * x_cols, (c + 1) * x_cols)
+            nc.vector.tensor_copy(
+                out=by_pass[:, :, c * per_load : (c + 1) * per_load, :],
+                in_=x_raw[:, cols].rearrange("p (a j e) -> p j a e", a=per_load, e=BLOCK),
+            )
+        x_pairs = x_sorted[:].bitcast(F32)
 
-        x_codes = keep.tile([P, GROUPS * P], U32, align_bytes=64)
-        x_scales = keep.tile([P, GROUPS * P], U8, align_bytes=64)
+        x_codes = keep.tile([P, PASSES * P], U32, align_bytes=64)
+        x_scales = keep.tile([P, PASSES * P], U8, align_bytes=64)
 
         def transpose_and_quantise(unit):
             turned = psum_t.tile([P, UNIT * 2 * P], F32)
             for i in range(UNIT):
-                g = unit * UNIT + i
+                j = unit * UNIT + i
                 for u in range(2):
                     at = (i * 2 + u) * P
                     nc.tensor.transpose(
                         out=turned[:, at : at + P],
-                        in_=x_pairs[:, 256 * g + u : 256 * (g + 1) : 2],
+                        in_=x_pairs[:, 256 * j + u : 256 * (j + 1) : 2],
                         identity=ident[:],
                     )
             grouped = stage.tile([P, UNIT * P * 4], BF16, align_bytes=64)
@@ -168,27 +174,27 @@ def tile_retnet_pa_k_kernel(
         loaded = {}
 
         def load_words(step):
-            w, chunk = divmod(step, CHUNKS)
-            words = ring.tile([P, CHUNK, 2 * WIDTH], U8, align_bytes=64)
-            src = words_in[w][chunk * CHUNK : (chunk + 1) * CHUNK].bitcast(I32)
-            nc.sync.dma_start(out=words[:].bitcast(I32), in_=src.rearrange("g p n -> p g n"))
+            w, j = divmod(step, PASSES)
+            words = ring.tile([P, 2 * WIDTH], U8, align_bytes=64)
+            rows = words_in[w].bitcast(I32).rearrange("g p n -> (g p) n")
+            rows = rows.rearrange("(a j s) n -> j a s n", a=STRETCHES, j=PASSES)
+            nc.sync.dma_start(out=words[:].bitcast(I32), in_=rows[j])
             loaded[step] = words
 
         def multiply(step):
-            w, chunk = divmod(step, CHUNKS)
+            w, j = divmod(step, PASSES)
             words = loaded[step]
             for b in range(BANKS):
-                for i in range(CHUNK):
-                    g = chunk * CHUNK + i
-                    nc.tensor.matmul_mx(
-                        out=acc[w][b][:],
-                        lhsT=x_codes[:, g * P : (g + 1) * P].bitcast(FP8X4),
-                        lhsT_scale=x_scales[:, g * P : (g + 1) * P],
-                        rhs=words[:, i, b * 2 * N_PASS : (b + 1) * 2 * N_PASS].bitcast(FP4X4),
-                        rhs_scale=planes[w][:, g, b * N_PASS : (b + 1) * N_PASS],
-                        start=(g == 0),
-                        stop=(g == GROUPS - 1),
-                    )
+                at = j * WIDTH + b * N_PASS
+                nc.tensor.matmul_mx(
+                    out=acc[w][b][:],
+                    lhsT=x_codes[:, j * P : (j + 1) * P].bitcast(FP8X4),
+                    lhsT_scale=x_scales[:, j * P : (j + 1) * P],
+                    rhs=words[:, b * 2 * N_PASS : (b + 1) * 2 * N_PASS].bitcast(FP4X4),
+                    rhs_scale=planes[w][:, at : at + N_PASS],
+                    start=(j == 0),
+                    stop=(j == PASSES - 1),
+                )
 
         def rotate_and_store(w, b):
             t = acc[w][b][:]
@@ -223,14 +229,14 @@ def tile_retnet_pa_k_kernel(
 
         ahead = RING - 1
         load_scales(0)
-        for step in range(2 * CHUNKS + ahead):
-            if step == CHUNKS // 2:
+        for step in range(2 * PASSES + ahead):
+            if step == PASSES // 2:
                 load_scales(1)
-            if step < 2 * CHUNKS:
+            if step < 2 * PASSES:
                 load_words(step)
             done = step - ahead
             if done >= 0:
                 multiply(done)
-                if done % CHUNKS == CHUNKS - 1:
+                if done % PASSES == PASSES - 1:
                     for b in range(BANKS):
-                        rotate_and_store(done // CHUNKS, b)
+                        rotate_and_store(done // PASSES, b)

@@ -16,10 +16,8 @@ ACT = mybir.ActivationFunctionType
 
 P = 128
 E = 16384
-BLOCK = 32
 K_PASS = 512
-PASSES = E // K_PASS
-STRETCHES = K_PASS // BLOCK
+GROUPS = E // K_PASS
 WIDTH = 1024
 N_PASS = 512
 BANKS = WIDTH // N_PASS
@@ -29,8 +27,11 @@ PAIRS = HEAD // 2
 
 X_LOADS = 8
 UNIT = 2
-UNITS = PASSES // UNIT
-RING = 24
+UNITS = GROUPS // UNIT
+CHUNK = 2
+CHUNKS = GROUPS // CHUNK
+RING = 18
+BLOCKS = K_PASS // 32
 
 FLOPS = 2 * P * E * 2 * WIDTH
 
@@ -62,47 +63,46 @@ def tile_retnet_pa_k_kernel(
         pos_int = keep.tile([P, 1], I32)
         nc.gpsimd.iota(pos_int[:], pattern=[[0, 1]], base=0, channel_multiplier=1)
 
-        planes = []
-        for w in range(2):
-            plane = keep.tile([P, PASSES * WIDTH], U8, align_bytes=64, name="plane%d" % w)
-            nc.vector.memset(plane[:].bitcast(I32), 0)
-            planes.append(plane)
+        planes = [
+            keep.tile([P, GROUPS, WIDTH], U8, align_bytes=64, name="plane%d" % w)
+            for w in range(2)
+        ]
+        nc.vector.memset(planes[0][:].bitcast(I32), 0)
 
-        def load_scales(w):
-            rows = scales_in[w].bitcast(I32).rearrange("g q n -> (g q) n")
-            rows = rows.rearrange("(h a j) n -> a h (j n)", h=2, j=PASSES)
-            for a in range(STRETCHES // 2):
-                first = 32 * (a // 4) + a % 4
-                nc.sync.dma_start(out=planes[w][first:P:64, :].bitcast(I32), in_=rows[a])
+        def load_wq_scales():
+            rows = scales_in[0].bitcast(I32).rearrange("g q n -> q g n")
+            for i in range(BLOCKS):
+                q = (i % 2) * (BLOCKS // 2) + i // 2
+                at = 32 * (q // 4) + q % 4
+                nc.sync.dma_start(
+                    out=planes[0][at : at + 1, :, :].bitcast(I32), in_=rows[q : q + 1]
+                )
+
+        def load_wk_scales():
+            rows = scales_in[1].bitcast(F32).rearrange("g (h q) n -> q h g n", h=2)
+            for q in range(BLOCKS // 2):
+                at = 32 * (q // 4) + q % 4
+                nc.gpsimd.dma_start(out=planes[1][at:P:64, :, :].bitcast(F32), in_=rows[q])
 
         x_raw = keep.tile([P, E], BF16)
-        x_sorted = keep.tile([P, E], BF16)
-        by_pass = x_sorted[:].rearrange("p (j a e) -> p j a e", j=PASSES, e=BLOCK)
-        x_cols = E // X_LOADS
-        per_load = STRETCHES // X_LOADS
-        for c in range(X_LOADS):
-            cols = slice(c * x_cols, (c + 1) * x_cols)
+        x_block = E // X_LOADS
+        for j in range(X_LOADS):
+            cols = slice(j * x_block, (j + 1) * x_block)
             nc.sync.dma_start(out=x_raw[:, cols], in_=x[0, :, cols])
-        for c in range(X_LOADS):
-            cols = slice(c * x_cols, (c + 1) * x_cols)
-            nc.vector.tensor_copy(
-                out=by_pass[:, :, c * per_load : (c + 1) * per_load, :],
-                in_=x_raw[:, cols].rearrange("p (a j e) -> p j a e", a=per_load, e=BLOCK),
-            )
-        x_pairs = x_sorted[:].bitcast(F32)
+        x_pairs = x_raw[:].bitcast(F32)
 
-        x_codes = keep.tile([P, PASSES * P], U32, align_bytes=64)
-        x_scales = keep.tile([P, PASSES * P], U8, align_bytes=64)
+        x_codes = keep.tile([P, GROUPS * P], U32, align_bytes=64)
+        x_scales = keep.tile([P, GROUPS * P], U8, align_bytes=64)
 
         def transpose_and_quantise(unit):
             turned = psum_t.tile([P, UNIT * 2 * P], F32)
             for i in range(UNIT):
-                j = unit * UNIT + i
+                g = unit * UNIT + i
                 for u in range(2):
                     at = (i * 2 + u) * P
                     nc.tensor.transpose(
                         out=turned[:, at : at + P],
-                        in_=x_pairs[:, 256 * j + u : 256 * (j + 1) : 2],
+                        in_=x_pairs[:, 256 * g + u : 256 * (g + 1) : 2],
                         identity=ident[:],
                     )
             grouped = stage.tile([P, UNIT * P * 4], BF16, align_bytes=64)
@@ -167,6 +167,9 @@ def tile_retnet_pa_k_kernel(
             sin_tab.append(sin_w)
             neg_sin_tab.append(neg_w)
 
+        nc.vector.memset(planes[1][:].bitcast(I32), 0)
+        load_wk_scales()
+
         acc = [
             [psum_acc.tile([P, N_PASS], F32, name="acc%d%d" % (w, b)) for b in range(BANKS)]
             for w in range(2)
@@ -174,27 +177,27 @@ def tile_retnet_pa_k_kernel(
         loaded = {}
 
         def load_words(step):
-            w, j = divmod(step, PASSES)
-            words = ring.tile([P, 2 * WIDTH], U8, align_bytes=64)
-            rows = words_in[w].bitcast(I32).rearrange("g p n -> (g p) n")
-            rows = rows.rearrange("(a j s) n -> j a s n", a=STRETCHES, j=PASSES)
-            nc.sync.dma_start(out=words[:].bitcast(I32), in_=rows[j])
+            w, chunk = divmod(step, CHUNKS)
+            words = ring.tile([P, CHUNK, 2 * WIDTH], U8, align_bytes=64)
+            src = words_in[w][chunk * CHUNK : (chunk + 1) * CHUNK].bitcast(I32)
+            nc.sync.dma_start(out=words[:].bitcast(I32), in_=src.rearrange("g p n -> p g n"))
             loaded[step] = words
 
         def multiply(step):
-            w, j = divmod(step, PASSES)
+            w, chunk = divmod(step, CHUNKS)
             words = loaded[step]
             for b in range(BANKS):
-                at = j * WIDTH + b * N_PASS
-                nc.tensor.matmul_mx(
-                    out=acc[w][b][:],
-                    lhsT=x_codes[:, j * P : (j + 1) * P].bitcast(FP8X4),
-                    lhsT_scale=x_scales[:, j * P : (j + 1) * P],
-                    rhs=words[:, b * 2 * N_PASS : (b + 1) * 2 * N_PASS].bitcast(FP4X4),
-                    rhs_scale=planes[w][:, at : at + N_PASS],
-                    start=(j == 0),
-                    stop=(j == PASSES - 1),
-                )
+                for i in range(CHUNK):
+                    g = chunk * CHUNK + i
+                    nc.tensor.matmul_mx(
+                        out=acc[w][b][:],
+                        lhsT=x_codes[:, g * P : (g + 1) * P].bitcast(FP8X4),
+                        lhsT_scale=x_scales[:, g * P : (g + 1) * P],
+                        rhs=words[:, i, b * 2 * N_PASS : (b + 1) * 2 * N_PASS].bitcast(FP4X4),
+                        rhs_scale=planes[w][:, g, b * N_PASS : (b + 1) * N_PASS],
+                        start=(g == 0),
+                        stop=(g == GROUPS - 1),
+                    )
 
         def rotate_and_store(w, b):
             t = acc[w][b][:]
@@ -228,15 +231,13 @@ def tile_retnet_pa_k_kernel(
             )
 
         ahead = RING - 1
-        load_scales(0)
-        for step in range(2 * PASSES + ahead):
-            if step == PASSES // 2:
-                load_scales(1)
-            if step < 2 * PASSES:
+        load_wq_scales()
+        for step in range(2 * CHUNKS + ahead):
+            if step < 2 * CHUNKS:
                 load_words(step)
             done = step - ahead
             if done >= 0:
                 multiply(done)
-                if done % PASSES == PASSES - 1:
+                if done % CHUNKS == CHUNKS - 1:
                     for b in range(BANKS):
-                        rotate_and_store(done // PASSES, b)
+                        rotate_and_store(done // CHUNKS, b)

@@ -54,6 +54,7 @@ def tile_retnet_pa_k_kernel(
         stage = stack.enter_context(tc.tile_pool(name="stage", bufs=4))
         ring = stack.enter_context(tc.tile_pool(name="ring", bufs=RING))
         work = stack.enter_context(tc.tile_pool(name="work", bufs=2))
+        results = stack.enter_context(tc.tile_pool(name="results", bufs=2 * BANKS))
         psum_t = stack.enter_context(tc.psum_pool(name="psum_t", bufs=4))
         psum_acc = stack.enter_context(tc.psum_pool(name="psum_acc", bufs=1))
         stack.enter_context(tc.manual_schedule())
@@ -63,26 +64,20 @@ def tile_retnet_pa_k_kernel(
         pos_int = keep.tile([P, 1], I32)
         nc.gpsimd.iota(pos_int[:], pattern=[[0, 1]], base=0, channel_multiplier=1)
 
-        planes = [
-            keep.tile([P, GROUPS, WIDTH], U8, align_bytes=64, name="plane%d" % w)
-            for w in range(2)
-        ]
-        nc.vector.memset(planes[0][:].bitcast(I32), 0)
+        planes = []
+        for w in range(2):
+            plane = keep.tile([P, GROUPS, WIDTH], U8, align_bytes=64, name="plane%d" % w)
+            nc.vector.memset(plane[:].bitcast(I32), 0)
+            planes.append(plane)
 
-        def load_wq_scales():
-            rows = scales_in[0].bitcast(I32).rearrange("g q n -> q g n")
+        def load_scales(w):
+            rows = scales_in[w].bitcast(I32).rearrange("g q n -> q g n")
             for i in range(BLOCKS):
                 q = (i % 2) * (BLOCKS // 2) + i // 2
                 at = 32 * (q // 4) + q % 4
                 nc.sync.dma_start(
-                    out=planes[0][at : at + 1, :, :].bitcast(I32), in_=rows[q : q + 1]
+                    out=planes[w][at : at + 1, :, :].bitcast(I32), in_=rows[q : q + 1]
                 )
-
-        def load_wk_scales():
-            rows = scales_in[1].bitcast(F32).rearrange("g (h q) n -> q h g n", h=2)
-            for q in range(BLOCKS // 2):
-                at = 32 * (q // 4) + q % 4
-                nc.gpsimd.dma_start(out=planes[1][at:P:64, :, :].bitcast(F32), in_=rows[q])
 
         x_raw = keep.tile([P, E], BF16)
         x_block = E // X_LOADS
@@ -167,9 +162,6 @@ def tile_retnet_pa_k_kernel(
             sin_tab.append(sin_w)
             neg_sin_tab.append(neg_w)
 
-        nc.vector.memset(planes[1][:].bitcast(I32), 0)
-        load_wk_scales()
-
         acc = [
             [psum_acc.tile([P, N_PASS], F32, name="acc%d%d" % (w, b)) for b in range(BANKS)]
             for w in range(2)
@@ -217,7 +209,7 @@ def tile_retnet_pa_k_kernel(
                     in1=table[:].unsqueeze(1).to_broadcast([P, HEADS_PER_BANK, PAIRS]),
                     op=ALU.mult,
                 )
-            rotated = work.tile([P, N_PASS], F32)
+            rotated = results.tile([P, N_PASS], F32)
             nc.vector.tensor_tensor(
                 out=rotated[:].rearrange("p (m e) -> p m e", e=2),
                 in0=direct[:].rearrange("p (m e) -> p m e", e=2),
@@ -225,14 +217,16 @@ def tile_retnet_pa_k_kernel(
                 op=ALU.add,
             )
             heads = slice(b * HEADS_PER_BANK, (b + 1) * HEADS_PER_BANK)
-            nc.scalar.dma_start(
+            nc.sync.dma_start(
                 out=outs[w][0, heads].rearrange("h i f -> i h f"),
                 in_=rotated[:].rearrange("p (h f) -> p h f", h=HEADS_PER_BANK),
             )
 
         ahead = RING - 1
-        load_wq_scales()
+        load_scales(0)
         for step in range(2 * CHUNKS + ahead):
+            if step == CHUNKS // 2:
+                load_scales(1)
             if step < 2 * CHUNKS:
                 load_words(step)
             done = step - ahead

@@ -66,7 +66,7 @@ def tile_retnet_pa_k_kernel(
 
         planes = []
         for w in range(2):
-            plane = keep.tile([P, GROUPS, WIDTH], U8, align_bytes=64, name="plane%d" % w)
+            plane = keep.tile([P, GROUPS, WIDTH], U8, align_bytes=4096, name="plane%d" % w)
             nc.vector.memset(plane[:].bitcast(I32), 0)
             planes.append(plane)
 
@@ -79,7 +79,7 @@ def tile_retnet_pa_k_kernel(
                     out=planes[w][at : at + 1, :, :].bitcast(I32), in_=rows[q : q + 1]
                 )
 
-        x_raw = keep.tile([P, E], BF16)
+        x_raw = keep.tile([P, E], BF16, align_bytes=4096)
         x_block = E // X_LOADS
         for j in range(X_LOADS):
             cols = slice(j * x_block, (j + 1) * x_block)
@@ -170,7 +170,7 @@ def tile_retnet_pa_k_kernel(
 
         def load_words(step):
             w, chunk = divmod(step, CHUNKS)
-            words = ring.tile([P, CHUNK, 2 * WIDTH], U8, align_bytes=64)
+            words = ring.tile([P, CHUNK, 2 * WIDTH], U8, align_bytes=4096)
             src = words_in[w][chunk * CHUNK : (chunk + 1) * CHUNK].bitcast(I32)
             nc.sync.dma_start(out=words[:].bitcast(I32), in_=src.rearrange("g p n -> p g n"))
             loaded[step] = words
@@ -209,7 +209,7 @@ def tile_retnet_pa_k_kernel(
                     in1=table[:].unsqueeze(1).to_broadcast([P, HEADS_PER_BANK, PAIRS]),
                     op=ALU.mult,
                 )
-            rotated = results.tile([P, N_PASS], F32)
+            rotated = results.tile([P, N_PASS], F32, align_bytes=2048)
             nc.vector.tensor_tensor(
                 out=rotated[:].rearrange("p (m e) -> p m e", e=2),
                 in0=direct[:].rearrange("p (m e) -> p m e", e=2),

@@ -66,7 +66,7 @@ def tile_retnet_pa_k_kernel(
 
         planes = []
         for w in range(2):
-            plane = keep.tile([P, GROUPS, WIDTH], U8, align_bytes=4096, name="plane%d" % w)
+            plane = keep.tile([P, GROUPS, WIDTH], U8, align_bytes=256, name="plane%d" % w)
             nc.vector.memset(plane[:].bitcast(I32), 0)
             planes.append(plane)
 
@@ -79,7 +79,7 @@ def tile_retnet_pa_k_kernel(
                     out=planes[w][at : at + 1, :, :].bitcast(I32), in_=rows[q : q + 1]
                 )
 
-        x_raw = keep.tile([P, E], BF16, align_bytes=4096)
+        x_raw = keep.tile([P, E], BF16, align_bytes=256)
         x_block = E // X_LOADS
         for j in range(X_LOADS):
             cols = slice(j * x_block, (j + 1) * x_block)
@@ -170,7 +170,7 @@ def tile_retnet_pa_k_kernel(
 
         def load_words(step):
             w, chunk = divmod(step, CHUNKS)
-            words = ring.tile([P, CHUNK, 2 * WIDTH], U8, align_bytes=4096)
+            words = ring.tile([P, CHUNK, 2 * WIDTH], U8, align_bytes=256)
             src = words_in[w][chunk * CHUNK : (chunk + 1) * CHUNK].bitcast(I32)
             nc.sync.dma_start(out=words[:].bitcast(I32), in_=src.rearrange("g p n -> p g n"))
             loaded[step] = words
@@ -209,7 +209,7 @@ def tile_retnet_pa_k_kernel(
                     in1=table[:].unsqueeze(1).to_broadcast([P, HEADS_PER_BANK, PAIRS]),
                     op=ALU.mult,
                 )
-            rotated = results.tile([P, N_PASS], F32, align_bytes=2048)
+            rotated = results.tile([P, N_PASS], F32, align_bytes=256)
             nc.vector.tensor_tensor(
                 out=rotated[:].rearrange("p (m e) -> p m e", e=2),
                 in0=direct[:].rearrange("p (m e) -> p m e", e=2),

@@ -25,7 +25,7 @@ HEAD = 128
 HEADS_PER_BANK = N_PASS // HEAD
 PAIRS = HEAD // 2
 
-X_LOADS = 8
+X_LOADS = 2
 UNIT = 2
 UNITS = GROUPS // UNIT
 CHUNK = 2
@@ -210,7 +210,8 @@ def tile_retnet_pa_k_kernel(
                     op=ALU.mult,
                 )
             rotated = results.tile([P, N_PASS], F32, align_bytes=256)
-            nc.vector.tensor_tensor(
+            adder = nc.gpsimd if b == 0 else nc.vector
+            adder.tensor_tensor(
                 out=rotated[:].rearrange("p (m e) -> p m e", e=2),
                 in0=direct[:].rearrange("p (m e) -> p m e", e=2),
                 in1=crossed[:].rearrange("p e m -> p m e"),
@@ -225,7 +226,7 @@ def tile_retnet_pa_k_kernel(
         ahead = RING - 1
         load_scales(0)
         for step in range(2 * CHUNKS + ahead):
-            if step == CHUNKS // 2:
+            if step == CHUNKS:
                 load_scales(1)
             if step < 2 * CHUNKS:
                 load_words(step)

@@ -73,8 +73,8 @@ def tile_retnet_pa_k_kernel(
         def load_scales(w):
             rows = scales_in[w].bitcast(I32).rearrange("g q n -> q g n")
             for i in range(BLOCKS):
-                q = (i % 2) * (BLOCKS // 2) + i // 2
-                at = 32 * (q // 4) + q % 4
+                at = 64 * (i % 2) + 32 * (i // 2 % 2) + i // 4
+                q = 4 * (at // 32) + at % 32
                 nc.sync.dma_start(
                     out=planes[w][at : at + 1, :, :].bitcast(I32), in_=rows[q : q + 1]
                 )

import math
from contextlib import ExitStack

import concourse.mybir as mybir
from concourse.masks import make_identity

F32 = mybir.dt.float32
BF16 = mybir.dt.bfloat16
I32 = mybir.dt.int32
U32 = mybir.dt.uint32
U8 = mybir.dt.uint8
FP8X4 = mybir.dt.float8_e4m3fn_x4
FP4X4 = mybir.dt.float4_e2m1fn_x4
ALU = mybir.AluOpType
ACT = mybir.ActivationFunctionType

P = 128
E = 16384
K_PASS = 512
GROUPS = E // K_PASS
WIDTH = 1024
N_PASS = 512
BANKS = WIDTH // N_PASS
HEAD = 128
HEADS_PER_BANK = N_PASS // HEAD
PAIRS = HEAD // 2

X_LOADS = 2
UNIT = 2
UNITS = GROUPS // UNIT
CHUNK = 2
CHUNKS = GROUPS // CHUNK
RING = 18
BLOCKS = K_PASS // 32

FLOPS = 2 * P * E * 2 * WIDTH

ROUND_MAGIC = 12582912.0
TURN_HI = 6.28125
TURN_LO = 2.0 * math.pi - TURN_HI


def tile_retnet_pa_k_kernel(
    tc, x, wq_words, wq_scales, wk_words, wk_scales, out_0, out_1
):
    nc = tc.nc
    words_in = (wq_words, wk_words)
    scales_in = (wq_scales, wk_scales)
    outs = (out_0, out_1)
    factors = (1.0, HEAD**-0.5)

    with ExitStack() as stack:
        keep = stack.enter_context(tc.tile_pool(name="keep", bufs=1))
        stage = stack.enter_context(tc.tile_pool(name="stage", bufs=4))
        ring = stack.enter_context(tc.tile_pool(name="ring", bufs=RING))
        work = stack.enter_context(tc.tile_pool(name="work", bufs=2))
        results = stack.enter_context(tc.tile_pool(name="results", bufs=2 * BANKS))
        psum_t = stack.enter_context(tc.psum_pool(name="psum_t", bufs=4))
        psum_acc = stack.enter_context(tc.psum_pool(name="psum_acc", bufs=1))
        stack.enter_context(tc.manual_schedule())

        ident = keep.tile([P, P], F32)
        make_identity(nc, ident[:])
        pos_int = keep.tile([P, 1], I32)
        nc.gpsimd.iota(pos_int[:], pattern=[[0, 1]], base=0, channel_multiplier=1)

        planes = []
        for w in range(2):
            plane = keep.tile([P, GROUPS, WIDTH], U8, align_bytes=256, name="plane%d" % w)
            nc.vector.memset(plane[:].bitcast(I32), 0)
            planes.append(plane)

        def load_scales(w):
            rows = scales_in[w].bitcast(I32).rearrange("g q n -> q g n")
            for i in range(BLOCKS):
                at = 64 * (i % 2) + 32 * (i // 2 % 2) + i // 4
                q = 4 * (at // 32) + at % 32
                nc.sync.dma_start(
                    out=planes[w][at : at + 1, :, :].bitcast(I32), in_=rows[q : q + 1]
                )

        x_raw = keep.tile([P, E], BF16, align_bytes=256)
        x_block = E // X_LOADS
        for j in range(X_LOADS):
            cols = slice(j * x_block, (j + 1) * x_block)
            nc.sync.dma_start(out=x_raw[:, cols], in_=x[0, :, cols])
        x_pairs = x_raw[:].bitcast(F32)

        x_codes = keep.tile([P, GROUPS * P], U32, align_bytes=64)
        x_scales = keep.tile([P, GROUPS * P], U8, align_bytes=64)

        def transpose_and_quantise(unit):
            turned = psum_t.tile([P, UNIT * 2 * P], F32)
            for i in range(UNIT):
                g = unit * UNIT + i
                for u in range(2):
                    at = (i * 2 + u) * P
                    nc.tensor.transpose(
                        out=turned[:, at : at + P],
                        in_=x_pairs[:, 256 * g + u : 256 * (g + 1) : 2],
                        identity=ident[:],
                    )
            grouped = stage.tile([P, UNIT * P * 4], BF16, align_bytes=64)
            nc.scalar.copy(
                out=grouped[:].bitcast(F32).rearrange("p (i r u) -> p i r u", i=UNIT, u=2),
                in_=turned[:].rearrange("p (i u r) -> p i r u", i=UNIT, u=2),
            )
            cols = slice(unit * UNIT * P, (unit + 1) * UNIT * P)
            nc.vector.quantize_mx(
                out=x_codes[:, cols].bitcast(FP8X4), scales=x_scales[:, cols], in_=grouped[:]
            )

        for unit in range(UNITS):
            transpose_and_quantise(unit)

        freq = keep.tile([P, PAIRS], F32)
        nc.vector.memset(freq[:], 1.0)
        for bit in range(6):
            step = 1 << bit
            odd = freq[:].rearrange("p (a two s) -> p a two s", two=2, s=step)[:, :, 1, :]
            nc.vector.tensor_scalar_mul(out=odd, in0=odd, scalar1=10000.0 ** (-step / 63.0))
        pos = keep.tile([P, 1], F32)
        nc.vector.tensor_copy(out=pos[:], in_=pos_int[:])
        angle = keep.tile([P, 2, PAIRS], F32)
        nc.vector.tensor_scalar_mul(out=angle[:, 0, :], in0=freq[:], scalar1=pos[:, 0:1])
        nc.vector.tensor_scalar(
            out=angle[:, 1, :], in0=freq[:], scalar1=pos[:, 0:1], scalar2=math.pi / 2,
            op0=ALU.mult, op1=ALU.add,
        )
        flat_angle = angle[:].rearrange("p a c -> p (a c)")
        turns = keep.tile([P, 2 * PAIRS], F32)
        nc.vector.tensor_scalar(
            out=turns[:], in0=flat_angle, scalar1=1.0 / (2.0 * math.pi), scalar2=ROUND_MAGIC,
            op0=ALU.mult, op1=ALU.add,
        )
        nc.vector.tensor_scalar_sub(out=turns[:], in0=turns[:], scalar1=ROUND_MAGIC)
        nc.vector.scalar_tensor_tensor(
            out=flat_angle, in0=turns[:], scalar=-TURN_HI, in1=flat_angle,
            op0=ALU.mult, op1=ALU.add,
        )
        nc.vector.scalar_tensor_tensor(
            out=flat_angle, in0=turns[:], scalar=-TURN_LO, in1=flat_angle,
            op0=ALU.mult, op1=ALU.add,
        )
        trig = keep.tile([P, 2, PAIRS], F32)
        nc.scalar.activation(
            out=trig[:].rearrange("p a c -> p (a c)"), in_=flat_angle, func=ACT.Sin
        )
        cos_tab, sin_tab, neg_sin_tab = [], [], []
        for w in range(2):
            cos_w = keep.tile([P, HEAD], F32, name="cos%d" % w)
            sin_w = keep.tile([P, PAIRS], F32, name="sin%d" % w)
            neg_w = keep.tile([P, PAIRS], F32, name="neg%d" % w)
            nc.vector.tensor_scalar_mul(
                out=cos_w[:].rearrange("p (c e) -> p c e", e=2),
                in0=trig[:, 1, :].unsqueeze(2).to_broadcast([P, PAIRS, 2]),
                scalar1=factors[w],
            )
            nc.vector.tensor_scalar_mul(out=sin_w[:], in0=trig[:, 0, :], scalar1=factors[w])
            nc.vector.tensor_scalar_mul(out=neg_w[:], in0=trig[:, 0, :], scalar1=-factors[w])
            cos_tab.append(cos_w)
            sin_tab.append(sin_w)
            neg_sin_tab.append(neg_w)

        acc = [
            [psum_acc.tile([P, N_PASS], F32, name="acc%d%d" % (w, b)) for b in range(BANKS)]
            for w in range(2)
        ]
        loaded = {}

        def load_words(step):
            w, chunk = divmod(step, CHUNKS)
            words = ring.tile([P, CHUNK, 2 * WIDTH], U8, align_bytes=256)
            src = words_in[w][chunk * CHUNK : (chunk + 1) * CHUNK].bitcast(I32)
            nc.sync.dma_start(out=words[:].bitcast(I32), in_=src.rearrange("g p n -> p g n"))
            loaded[step] = words

        def multiply(step):
            w, chunk = divmod(step, CHUNKS)
            words = loaded[step]
            for b in range(BANKS):
                for i in range(CHUNK):
                    g = chunk * CHUNK + i
                    nc.tensor.matmul_mx(
                        out=acc[w][b][:],
                        lhsT=x_codes[:, g * P : (g + 1) * P].bitcast(FP8X4),
                        lhsT_scale=x_scales[:, g * P : (g + 1) * P],
                        rhs=words[:, i, b * 2 * N_PASS : (b + 1) * 2 * N_PASS].bitcast(FP4X4),
                        rhs_scale=planes[w][:, g, b * N_PASS : (b + 1) * N_PASS],
                        start=(g == 0),
                        stop=(g == GROUPS - 1),
                    )

        def rotate_and_store(w, b):
            t = acc[w][b][:]
            by_pair = t.rearrange("p (h c e) -> p h c e", h=HEADS_PER_BANK, e=2)
            direct = work.tile([P, N_PASS], F32)
            nc.vector.tensor_tensor(
                out=direct[:].rearrange("p (h f) -> p h f", h=HEADS_PER_BANK),
                in0=t.rearrange("p (h f) -> p h f", h=HEADS_PER_BANK),
                in1=cos_tab[w][:].unsqueeze(1).to_broadcast([P, HEADS_PER_BANK, HEAD]),
                op=ALU.mult,
            )
            crossed = work.tile([P, 2, N_PASS // 2], F32)
            for e, table in ((0, neg_sin_tab[w]), (1, sin_tab[w])):
                nc.vector.tensor_tensor(
                    out=crossed[:, e, :].rearrange("p (h c) -> p h c", h=HEADS_PER_BANK),
                    in0=by_pair[:, :, :, 1 - e],
                    in1=table[:].unsqueeze(1).to_broadcast([P, HEADS_PER_BANK, PAIRS]),
                    op=ALU.mult,
                )
            rotated = results.tile([P, N_PASS], F32, align_bytes=256)
            adder = nc.gpsimd if b == 0 else nc.vector
            adder.tensor_tensor(
                out=rotated[:].rearrange("p (m e) -> p m e", e=2),
                in0=direct[:].rearrange("p (m e) -> p m e", e=2),
                in1=crossed[:].rearrange("p e m -> p m e"),
                op=ALU.add,
            )
            heads = slice(b * HEADS_PER_BANK, (b + 1) * HEADS_PER_BANK)
            nc.sync.dma_start(
                out=outs[w][0, heads].rearrange("h i f -> i h f"),
                in_=rotated[:].rearrange("p (h f) -> p h f", h=HEADS_PER_BANK),
            )

        ahead = RING - 1
        load_scales(0)
        for step in range(2 * CHUNKS + ahead):
            if step == CHUNKS:
                load_scales(1)
            if step < 2 * CHUNKS:
                load_words(step)
            done = step - ahead
            if done >= 0:
                multiply(done)
                if done % CHUNKS == CHUNKS - 1:
                    for b in range(BANKS):
                        rotate_and_store(done // CHUNKS, b)
